import numpy as np
import ml_dtypes

BF16 = ml_dtypes.bfloat16


def bf(x):
    return np.asarray(x, np.float32).astype(BF16)


def f32(x):
    return np.asarray(x, np.float32)


def f64(x):
    return np.asarray(x).astype(np.float64)


def striped(idx):
    return np.tile(idx.reshape(-1, 16).T, (8, 1))


B, T, D, K, S, N = 2, 256, 256, 128, 512, 256
BN_EPS = 1e-5


def setup_inputs():
    sc = 1.0 / np.sqrt(D)
    return {
        "base": f32(0.3 * np.random.standard_normal((D, S))),
        "x": bf(np.random.standard_normal((D, B * T))),
        "clusters": bf(sc * np.random.standard_normal((D, K))),
        "clusters2": f32(sc * np.random.standard_normal((D, K))),
        "bn_gamma": f32(1.0 + 0.1 * np.random.standard_normal((K, 1))),
        "bn_beta": f32(0.1 * np.random.standard_normal((K, 1))),
        "offs": striped(np.random.permutation(S)[:N]),
    }


def reference(base, x, clusters, clusters2, bn_gamma, bn_beta, offs):
    idx = offs[:16].T.reshape(-1)
    xf = f64(x)
    z = f64(clusters).T @ xf
    mean = z.mean(axis=1, keepdims=True)
    var = ((z - mean) ** 2).mean(axis=1, keepdims=True)
    y = (z - mean) / np.sqrt(var + BN_EPS) * f64(bn_gamma) + f64(bn_beta)
    e = np.exp(y)
    asg = e / e.sum(axis=0, keepdims=True)
    res = f64(base).copy()
    for i in range(B):
        ab = asg[:, i * T:(i + 1) * T]
        agg = xf[:, i * T:(i + 1) * T] @ ab.T
        neg = -(ab.sum(axis=1)[None, :] * f64(clusters2))
        res[:, idx[i * K:(i + 1) * K]] = agg + neg
    return res

@@ -1,0 +1,146 @@
+import concourse.mybir as mybir
+from concourse.masks import make_identity
+
+F32, BF16, U16 = mybir.dt.float32, mybir.dt.bfloat16, mybir.dt.uint16
+ALU = mybir.AluOpType
+ACT = mybir.ActivationFunctionType
+AXIS = mybir.AxisListType
+
+P = 128
+SAMPLES = 2
+TOKENS = 512
+FEATURES = 256
+CLUSTERS = 128
+BANK = 512
+LISTED = 256
+BN_EPS = 1e-5
+
+FEATURE_BLOCKS = FEATURES // P
+TOKEN_BLOCKS = TOKENS // P
+BLOCKS_PER_SAMPLE = TOKEN_BLOCKS // SAMPLES
+
+FLOPS = 2 * 2 * FEATURES * CLUSTERS * TOKENS
+
+
+def tile_modelnew_kernel(tc, base, x, clusters, clusters2, bn_gamma, bn_beta, offs, out):
+    nc = tc.nc
+    feature_blocks = range(FEATURE_BLOCKS)
+    token_blocks = range(TOKEN_BLOCKS)
+
+    with (
+        tc.tile_pool(name="held", bufs=1) as held,
+        tc.tile_pool(name="per_block", bufs=TOKEN_BLOCKS) as per_block,
+        tc.psum_pool(name="flipped", bufs=TOKEN_BLOCKS) as flipped,
+    ):
+        offsets = held.tile([P, LISTED // 16], U16, name="offsets")
+        x_sb = [held.tile([P, TOKENS], BF16, name=f"x_sb{b}") for b in feature_blocks]
+        clusters_sb = [held.tile([P, CLUSTERS], BF16, name=f"clusters_sb{b}") for b in feature_blocks]
+        centres_sb = [held.tile([P, CLUSTERS], F32, name=f"centres_sb{b}") for b in feature_blocks]
+        window = [held.tile([P, BANK], F32, name=f"window{b}") for b in feature_blocks]
+        gamma = held.tile([P, 1], F32, name="gamma")
+        beta = held.tile([P, 1], F32, name="beta")
+
+        queues = [nc.sync, nc.scalar]
+        for b in feature_blocks:
+            rows = slice(b * P, (b + 1) * P)
+            queues[b].dma_start(clusters_sb[b][:], clusters[rows, :])
+            queues[b].dma_start(x_sb[b][:], x[rows, :])
+        nc.sync.dma_start(offsets[:], offs)
+        nc.scalar.dma_start(gamma[:], bn_gamma)
+        nc.scalar.dma_start(beta[:], bn_beta)
+        for b in feature_blocks:
+            rows = slice(b * P, (b + 1) * P)
+            nc.gpsimd.dma_start(centres_sb[b][:], clusters2[rows, :])
+            queues[b].dma_start(window[b][:], base[rows, :])
+
+        identity_bf16 = held.tile([P, P], BF16, name="identity_bf16")
+        identity_f32 = held.tile([P, P], F32, name="identity_f32")
+        ones = held.tile([P, P], BF16, name="ones")
+        minus_half = held.tile([P, 1], F32, name="minus_half")
+        make_identity(nc, identity_bf16[:])
+        make_identity(nc, identity_f32[:])
+        nc.gpsimd.memset(ones[:], 1.0)
+        nc.gpsimd.memset(minus_half[:], -0.5)
+        neg_centres = [held.tile([P, CLUSTERS], F32, name=f"neg_centres{b}") for b in feature_blocks]
+        for b in feature_blocks:
+            nc.gpsimd.tensor_scalar_mul(neg_centres[b][:], centres_sb[b][:], -1.0)
+
+        y_sb = held.tile([P, TOKENS], F32, name="y_sb")
+        xT_sb = held.tile([P, TOKEN_BLOCKS, FEATURES], BF16, name="xT_sb")
+        yT_ps = [flipped.tile([P, CLUSTERS], F32, name="yT_ps") for t in token_blocks]
+
+        with tc.psum_pool(name="front", bufs=1) as front:
+            z_ps = front.tile([P, TOKENS], F32, name="z_ps")
+            for b in feature_blocks:
+                nc.tensor.matmul(
+                    z_ps[:], clusters_sb[b][:], x_sb[b][:],
+                    start=(b == 0), stop=(b == FEATURE_BLOCKS - 1),
+                )
+
+            xT_ps = front.tile([P, TOKEN_BLOCKS, FEATURES], BF16, name="xT_ps")
+            for t in token_blocks:
+                for b in feature_blocks:
+                    nc.tensor.transpose(
+                        xT_ps[:, t, b * P : (b + 1) * P], x_sb[b][:, t * P : (t + 1) * P], identity_bf16[:]
+                    )
+            nc.scalar.copy(xT_sb[:], xT_ps[:])
+
+            stats = held.tile([P, 6], F32, name="stats")
+            mean_var = held.tile([P, 2], F32, name="mean_var")
+            nc.vector.bn_stats(stats[:], z_ps[:])
+            nc.vector.bn_aggr(mean_var[:], stats[:])
+            mean, var = mean_var[:, 0:1], mean_var[:, 1:2]
+            var_eps = held.tile([P, 1], F32, name="var_eps")
+            rstd = held.tile([P, 1], F32, name="rstd")
+            neg_mean_gamma = held.tile([P, 1], F32, name="neg_mean_gamma")
+            scale = held.tile([P, 1], F32, name="scale")
+            shift = held.tile([P, 1], F32, name="shift")
+            nc.vector.tensor_scalar_add(var_eps[:], var, BN_EPS)
+            nc.gpsimd.tensor_tensor(rstd[:], var_eps[:], minus_half[:], ALU.pow)
+            nc.vector.tensor_scalar(neg_mean_gamma[:], mean, gamma[:], -1.0, op0=ALU.mult, op1=ALU.mult)
+            nc.vector.tensor_mul(scale[:], gamma[:], rstd[:])
+            nc.vector.tensor_scalar(shift[:], neg_mean_gamma[:], rstd[:], beta[:], op0=ALU.mult, op1=ALU.add)
+
+            for t in token_blocks:
+                block = slice(t * P, (t + 1) * P)
+                nc.vector.tensor_scalar(y_sb[:, block], z_ps[:, block], scale[:], shift[:], op0=ALU.mult, op1=ALU.add)
+                nc.tensor.transpose(yT_ps[t][:], y_sb[:, block], identity_f32[:])
+
+        with tc.psum_pool(name="back", bufs=1) as back:
+            e_sb, e_sum, asgT = [], [], []
+            for t in token_blocks:
+                neg_max = per_block.tile([P, 1], F32, name="neg_max")
+                e_sb.append(per_block.tile([P, CLUSTERS], F32, name="e_sb"))
+                e_sum.append(per_block.tile([P, 1], F32, name="e_sum"))
+                nc.vector.tensor_reduce(neg_max[:], yT_ps[t][:], axis=AXIS.X, op=ALU.max, negate=True)
+                nc.scalar.activation(e_sb[t][:], yT_ps[t][:], ACT.Exp, bias=neg_max[:], accum_out=e_sum[t][:])
+            for t in token_blocks:
+                inv_sum = per_block.tile([P, 1], F32, name="inv_sum")
+                asgT.append(per_block.tile([P, CLUSTERS], BF16, name="asgT"))
+                nc.vector.reciprocal(inv_sum[:], e_sum[t][:])
+                nc.scalar.activation(asgT[t][:], e_sb[t][:], ACT.Copy, scale=inv_sum[:])
+
+            asum_ps = back.tile([P, LISTED], F32, name="asum_ps")
+            agg_ps = [back.tile([P, LISTED], F32, name=f"agg_ps{b}") for b in feature_blocks]
+            for t in token_blocks:
+                sample, step = divmod(t, BLOCKS_PER_SAMPLE)
+                columns = slice(sample * CLUSTERS, (sample + 1) * CLUSTERS)
+                first, last = step == 0, step == BLOCKS_PER_SAMPLE - 1
+                nc.tensor.matmul(asum_ps[:, columns], ones[:], asgT[t][:], start=first, stop=last)
+                for b in feature_blocks:
+                    nc.tensor.matmul(
+                        agg_ps[b][:, columns], xT_sb[:, t, b * P : (b + 1) * P], asgT[t][:], start=first, stop=last
+                    )
+
+            for b in feature_blocks:
+                neg = held.tile([P, LISTED], F32, name=f"neg{b}")
+                agg_sb = held.tile([P, LISTED], F32, name=f"agg_sb{b}")
+                nc.scalar.copy(agg_sb[:], agg_ps[b][:])
+                nc.vector.tensor_tensor(
+                    neg[:].rearrange("p (i k) -> p i k", i=SAMPLES),
+                    asum_ps[:].rearrange("p (i k) -> p i k", i=SAMPLES),
+                    neg_centres[b][:].unsqueeze(1).to_broadcast([P, SAMPLES, CLUSTERS]),
+                    ALU.mult,
+                )
+                nc.vector.tensor_tensor(window[b][:].indirect(offsets[:]), agg_sb[:], neg[:], ALU.add)
+                nc.sync.dma_start(out[b * P : (b + 1) * P, :], window[b][:])

@@ -50,20 +50,21 @@ def tile_modelnew_kernel(tc, base, x, clusters, clusters2, bn_gamma, bn_beta, of
         nc.scalar.dma_start(beta[:], bn_beta)
         for b in feature_blocks:
             rows = slice(b * P, (b + 1) * P)
-            nc.gpsimd.dma_start(centres_sb[b][:], clusters2[rows, :])
+            queues[b].dma_start(centres_sb[b][:], clusters2[rows, :])
             queues[b].dma_start(window[b][:], base[rows, :])
 
-        identity_bf16 = held.tile([P, P], BF16, name="identity_bf16")
         identity_f32 = held.tile([P, P], F32, name="identity_f32")
+        identity_bf16 = held.tile([P, P], BF16, name="identity_bf16")
         ones = held.tile([P, P], BF16, name="ones")
         minus_half = held.tile([P, 1], F32, name="minus_half")
-        make_identity(nc, identity_bf16[:])
         make_identity(nc, identity_f32[:])
-        nc.gpsimd.memset(ones[:], 1.0)
-        nc.gpsimd.memset(minus_half[:], -0.5)
+        nc.vector.tensor_copy(identity_bf16[:], identity_f32[:])
+        nc.vector.memset(ones[:], 1.0)
+        nc.vector.memset(minus_half[:], -0.5)
+
         neg_centres = [held.tile([P, CLUSTERS], F32, name=f"neg_centres{b}") for b in feature_blocks]
         for b in feature_blocks:
-            nc.gpsimd.tensor_scalar_mul(neg_centres[b][:], centres_sb[b][:], -1.0)
+            nc.scalar.mul(neg_centres[b][:], centres_sb[b][:], -1.0)
 
         y_sb = held.tile([P, TOKENS], F32, name="y_sb")
         xT_sb = held.tile([P, TOKEN_BLOCKS, FEATURES], BF16, name="xT_sb")

@@ -18,6 +18,7 @@ BN_EPS = 1e-5
 FEATURE_BLOCKS = FEATURES // P
 TOKEN_BLOCKS = TOKENS // P
 BLOCKS_PER_SAMPLE = TOKEN_BLOCKS // SAMPLES
+SAMPLE_TOKENS = TOKENS // SAMPLES
 
 FLOPS = 2 * 2 * FEATURES * CLUSTERS * TOKENS
 
@@ -26,6 +27,7 @@ def tile_modelnew_kernel(tc, base, x, clusters, clusters2, bn_gamma, bn_beta, of
     nc = tc.nc
     feature_blocks = range(FEATURE_BLOCKS)
     token_blocks = range(TOKEN_BLOCKS)
+    samples = range(SAMPLES)
 
     with (
         tc.tile_pool(name="held", bufs=1) as held,
@@ -71,12 +73,15 @@ def tile_modelnew_kernel(tc, base, x, clusters, clusters2, bn_gamma, bn_beta, of
         yT_ps = [flipped.tile([P, CLUSTERS], F32, name="yT_ps") for t in token_blocks]
 
         with tc.psum_pool(name="front", bufs=1) as front:
-            z_ps = front.tile([P, TOKENS], F32, name="z_ps")
-            for b in feature_blocks:
-                nc.tensor.matmul(
-                    z_ps[:], clusters_sb[b][:], x_sb[b][:],
-                    start=(b == 0), stop=(b == FEATURE_BLOCKS - 1),
-                )
+            z_ps = [front.tile([P, SAMPLE_TOKENS], F32, name=f"z_ps{i}") for i in samples]
+            stats = held.tile([P, SAMPLES, 6], F32, name="stats")
+            for i in samples:
+                for b in feature_blocks:
+                    nc.tensor.matmul(
+                        z_ps[i][:], clusters_sb[b][:], x_sb[b][:, i * SAMPLE_TOKENS : (i + 1) * SAMPLE_TOKENS],
+                        start=(b == 0), stop=(b == FEATURE_BLOCKS - 1),
+                    )
+                nc.vector.bn_stats(stats[:, i, :], z_ps[i][:])
 
             xT_ps = front.tile([P, TOKEN_BLOCKS, FEATURES], BF16, name="xT_ps")
             for t in token_blocks:
@@ -86,10 +91,8 @@ def tile_modelnew_kernel(tc, base, x, clusters, clusters2, bn_gamma, bn_beta, of
                     )
             nc.scalar.copy(xT_sb[:], xT_ps[:])
 
-            stats = held.tile([P, 6], F32, name="stats")
             mean_var = held.tile([P, 2], F32, name="mean_var")
-            nc.vector.bn_stats(stats[:], z_ps[:])
-            nc.vector.bn_aggr(mean_var[:], stats[:])
+            nc.vector.bn_aggr(mean_var[:], stats[:].rearrange("p i s -> p (i s)"))
             mean, var = mean_var[:, 0:1], mean_var[:, 1:2]
             var_eps = held.tile([P, 1], F32, name="var_eps")
             rstd = held.tile([P, 1], F32, name="rstd")
@@ -103,8 +106,12 @@ def tile_modelnew_kernel(tc, base, x, clusters, clusters2, bn_gamma, bn_beta, of
             nc.vector.tensor_scalar(shift[:], neg_mean_gamma[:], rstd[:], beta[:], op0=ALU.mult, op1=ALU.add)
 
             for t in token_blocks:
+                sample, step = divmod(t, BLOCKS_PER_SAMPLE)
                 block = slice(t * P, (t + 1) * P)
-                nc.vector.tensor_scalar(y_sb[:, block], z_ps[:, block], scale[:], shift[:], op0=ALU.mult, op1=ALU.add)
+                nc.vector.tensor_scalar(
+                    y_sb[:, block], z_ps[sample][:, step * P : (step + 1) * P], scale[:], shift[:],
+                    op0=ALU.mult, op1=ALU.add,
+                )
                 nc.tensor.transpose(yT_ps[t][:], y_sb[:, block], identity_f32[:])
 
         with tc.psum_pool(name="back", bufs=1) as back:
@@ -121,27 +128,24 @@ def tile_modelnew_kernel(tc, base, x, clusters, clusters2, bn_gamma, bn_beta, of
                 nc.vector.reciprocal(inv_sum[:], e_sum[t][:])
                 nc.scalar.activation(asgT[t][:], e_sb[t][:], ACT.Copy, scale=inv_sum[:])
 
-            asum_ps = back.tile([P, LISTED], F32, name="asum_ps")
+            asum_ps = [back.tile([P, CLUSTERS], F32, name=f"asum_ps{i}") for i in samples]
             agg_ps = [back.tile([P, LISTED], F32, name=f"agg_ps{b}") for b in feature_blocks]
+            neg = [held.tile([P, LISTED], F32, name=f"neg{b}") for b in feature_blocks]
             for t in token_blocks:
                 sample, step = divmod(t, BLOCKS_PER_SAMPLE)
                 columns = slice(sample * CLUSTERS, (sample + 1) * CLUSTERS)
                 first, last = step == 0, step == BLOCKS_PER_SAMPLE - 1
-                nc.tensor.matmul(asum_ps[:, columns], ones[:], asgT[t][:], start=first, stop=last)
+                nc.tensor.matmul(asum_ps[sample][:], ones[:], asgT[t][:], start=first, stop=last)
                 for b in feature_blocks:
                     nc.tensor.matmul(
                         agg_ps[b][:, columns], xT_sb[:, t, b * P : (b + 1) * P], asgT[t][:], start=first, stop=last
                     )
+                if last:
+                    for b in feature_blocks:
+                        nc.vector.tensor_mul(neg[b][:, columns], asum_ps[sample][:], neg_centres[b][:])
 
             for b in feature_blocks:
-                neg = held.tile([P, LISTED], F32, name=f"neg{b}")
                 agg_sb = held.tile([P, LISTED], F32, name=f"agg_sb{b}")
                 nc.scalar.copy(agg_sb[:], agg_ps[b][:])
-                nc.vector.tensor_tensor(
-                    neg[:].rearrange("p (i k) -> p i k", i=SAMPLES),
-                    asum_ps[:].rearrange("p (i k) -> p i k", i=SAMPLES),
-                    neg_centres[b][:].unsqueeze(1).to_broadcast([P, SAMPLES, CLUSTERS]),
-                    ALU.mult,
-                )
-                nc.vector.tensor_tensor(window[b][:].indirect(offsets[:]), agg_sb[:], neg[:], ALU.add)
+                nc.vector.tensor_tensor(window[b][:].indirect(offsets[:]), agg_sb[:], neg[b][:], ALU.add)
                 nc.sync.dma_start(out[b * P : (b + 1) * P, :], window[b][:])

@@ -20,6 +20,8 @@ TOKEN_BLOCKS = TOKENS // P
 BLOCKS_PER_SAMPLE = TOKEN_BLOCKS // SAMPLES
 SAMPLE_TOKENS = TOKENS // SAMPLES
 
+WARM_UP_MATMULS = 4
+
 FLOPS = 2 * 2 * FEATURES * CLUSTERS * TOKENS
 
 
@@ -59,10 +61,12 @@ def tile_modelnew_kernel(tc, base, x, clusters, clusters2, bn_gamma, bn_beta, of
         identity_bf16 = held.tile([P, P], BF16, name="identity_bf16")
         ones = held.tile([P, P], BF16, name="ones")
         minus_half = held.tile([P, 1], F32, name="minus_half")
-        make_identity(nc, identity_f32[:])
-        nc.vector.tensor_copy(identity_bf16[:], identity_f32[:])
+        zeros = held.tile([P, TOKENS], BF16, name="zeros")
+        nc.vector.memset(zeros[:], 0.0)
         nc.vector.memset(ones[:], 1.0)
         nc.vector.memset(minus_half[:], -0.5)
+        make_identity(nc, identity_f32[:])
+        nc.vector.tensor_copy(identity_bf16[:], identity_f32[:])
 
         neg_centres = [held.tile([P, CLUSTERS], F32, name=f"neg_centres{b}") for b in feature_blocks]
         for b in feature_blocks:
@@ -73,6 +77,10 @@ def tile_modelnew_kernel(tc, base, x, clusters, clusters2, bn_gamma, bn_beta, of
         yT_ps = [flipped.tile([P, CLUSTERS], F32, name="yT_ps") for t in token_blocks]
 
         with tc.psum_pool(name="front", bufs=1) as front:
+            idle_ps = front.tile([P, TOKENS], F32, name="idle_ps")
+            for r in range(WARM_UP_MATMULS):
+                nc.tensor.matmul(idle_ps[:], zeros[:, 0:P], zeros[:], start=True, stop=True)
+
             z_ps = [front.tile([P, SAMPLE_TOKENS], F32, name=f"z_ps{i}") for i in samples]
             stats = held.tile([P, SAMPLES, 6], F32, name="stats")
             for i in samples:

@@ -134,7 +134,7 @@ def tile_modelnew_kernel(tc, base, x, clusters, clusters2, bn_gamma, bn_beta, of
                 inv_sum = per_block.tile([P, 1], F32, name="inv_sum")
                 asgT.append(per_block.tile([P, CLUSTERS], BF16, name="asgT"))
                 nc.vector.reciprocal(inv_sum[:], e_sum[t][:])
-                nc.scalar.activation(asgT[t][:], e_sb[t][:], ACT.Copy, scale=inv_sum[:])
+                nc.vector.tensor_scalar_mul(asgT[t][:], e_sb[t][:], inv_sum[:])
 
             asum_ps = [back.tile([P, CLUSTERS], F32, name=f"asum_ps{i}") for i in samples]
             agg_ps = [back.tile([P, LISTED], F32, name=f"agg_ps{b}") for b in feature_blocks]

@@ -20,7 +20,7 @@ TOKEN_BLOCKS = TOKENS // P
 BLOCKS_PER_SAMPLE = TOKEN_BLOCKS // SAMPLES
 SAMPLE_TOKENS = TOKENS // SAMPLES
 
-WARM_UP_MATMULS = 4
+WARM_UP_MATMULS = 16
 
 FLOPS = 2 * 2 * FEATURES * CLUSTERS * TOKENS
 
@@ -61,8 +61,8 @@ def tile_modelnew_kernel(tc, base, x, clusters, clusters2, bn_gamma, bn_beta, of
         identity_bf16 = held.tile([P, P], BF16, name="identity_bf16")
         ones = held.tile([P, P], BF16, name="ones")
         minus_half = held.tile([P, 1], F32, name="minus_half")
-        zeros = held.tile([P, TOKENS], BF16, name="zeros")
-        nc.vector.memset(zeros[:], 0.0)
+        zeros = held.tile([P, P], BF16, name="zeros")
+        nc.gpsimd.memset(zeros[:], 0.0)
         nc.vector.memset(ones[:], 1.0)
         nc.vector.memset(minus_half[:], -0.5)
         make_identity(nc, identity_f32[:])
@@ -77,9 +77,9 @@ def tile_modelnew_kernel(tc, base, x, clusters, clusters2, bn_gamma, bn_beta, of
         yT_ps = [flipped.tile([P, CLUSTERS], F32, name="yT_ps") for t in token_blocks]
 
         with tc.psum_pool(name="front", bufs=1) as front:
-            idle_ps = front.tile([P, TOKENS], F32, name="idle_ps")
+            idle_ps = front.tile([P, P], F32, name="idle_ps")
             for r in range(WARM_UP_MATMULS):
-                nc.tensor.matmul(idle_ps[:], zeros[:, 0:P], zeros[:], start=True, stop=True)
+                nc.tensor.matmul(idle_ps[:], zeros[:], zeros[:], start=True, stop=True)
 
             z_ps = [front.tile([P, SAMPLE_TOKENS], F32, name=f"z_ps{i}") for i in samples]
             stats = held.tile([P, SAMPLES, 6], F32, name="stats")

@@ -139,18 +139,24 @@ def tile_modelnew_kernel(tc, base, x, clusters, clusters2, bn_gamma, bn_beta, of
             asum_ps = [back.tile([P, CLUSTERS], F32, name=f"asum_ps{i}") for i in samples]
             agg_ps = [back.tile([P, LISTED], F32, name=f"agg_ps{b}") for b in feature_blocks]
             neg = [held.tile([P, LISTED], F32, name=f"neg{b}") for b in feature_blocks]
+            def agg_matmul(b, t):
+                sample, step = divmod(t, BLOCKS_PER_SAMPLE)
+                nc.tensor.matmul(
+                    agg_ps[b][:, sample * CLUSTERS : (sample + 1) * CLUSTERS], xT_sb[:, t, b * P : (b + 1) * P], asgT[t][:],
+                    start=(step == 0), stop=(step == BLOCKS_PER_SAMPLE - 1),
+                )
+
             for t in token_blocks:
                 sample, step = divmod(t, BLOCKS_PER_SAMPLE)
                 columns = slice(sample * CLUSTERS, (sample + 1) * CLUSTERS)
                 first, last = step == 0, step == BLOCKS_PER_SAMPLE - 1
                 nc.tensor.matmul(asum_ps[sample][:], ones[:], asgT[t][:], start=first, stop=last)
-                for b in feature_blocks:
-                    nc.tensor.matmul(
-                        agg_ps[b][:, columns], xT_sb[:, t, b * P : (b + 1) * P], asgT[t][:], start=first, stop=last
-                    )
+                agg_matmul(0, t)
                 if last:
                     for b in feature_blocks:
                         nc.vector.tensor_mul(neg[b][:, columns], asum_ps[sample][:], neg_centres[b][:])
+            for t in token_blocks:
+                agg_matmul(1, t)
 
             for b in feature_blocks:
                 agg_sb = held.tile([P, LISTED], F32, name=f"agg_sb{b}")

@@ -21,6 +21,7 @@ BLOCKS_PER_SAMPLE = TOKEN_BLOCKS // SAMPLES
 SAMPLE_TOKENS = TOKENS // SAMPLES
 
 WARM_UP_MATMULS = 16
+KEEP_WARM_MATMULS = 8
 
 FLOPS = 2 * 2 * FEATURES * CLUSTERS * TOKENS
 
@@ -121,6 +122,9 @@ def tile_modelnew_kernel(tc, base, x, clusters, clusters2, bn_gamma, bn_beta, of
                     op0=ALU.mult, op1=ALU.add,
                 )
                 nc.tensor.transpose(yT_ps[t][:], y_sb[:, block], identity_f32[:])
+
+            for r in range(KEEP_WARM_MATMULS):
+                nc.tensor.matmul(idle_ps[:], zeros[:], xT_sb[:, 0, 0:P], start=True, stop=True)
 
         with tc.psum_pool(name="back", bufs=1) as back:
             e_sb, e_sum, asgT = [], [], []

@@ -42,8 +42,10 @@ def tile_modelnew_kernel(tc, base, x, clusters, clusters2, bn_gamma, bn_beta, of
         clusters_sb = [held.tile([P, CLUSTERS], BF16, name=f"clusters_sb{b}") for b in feature_blocks]
         centres_sb = [held.tile([P, CLUSTERS], F32, name=f"centres_sb{b}") for b in feature_blocks]
         window = [held.tile([P, BANK], F32, name=f"window{b}") for b in feature_blocks]
-        gamma = held.tile([P, 1], F32, name="gamma")
-        beta = held.tile([P, 1], F32, name="beta")
+        factors = held.tile([P, 2], F32, name="factors")
+        addends = held.tile([P, 2], F32, name="addends")
+        gamma, neg_mean_gamma = factors[:, 0:1], factors[:, 1:2]
+        nc.vector.memset(addends[:], 0.0)
 
         queues = [nc.sync, nc.scalar]
         for b in feature_blocks:
@@ -51,8 +53,8 @@ def tile_modelnew_kernel(tc, base, x, clusters, clusters2, bn_gamma, bn_beta, of
             queues[b].dma_start(clusters_sb[b][:], clusters[rows, :])
             queues[b].dma_start(x_sb[b][:], x[rows, :])
         nc.sync.dma_start(offsets[:], offs)
-        nc.scalar.dma_start(gamma[:], bn_gamma)
-        nc.scalar.dma_start(beta[:], bn_beta)
+        nc.scalar.dma_start(gamma, bn_gamma)
+        nc.scalar.dma_start(addends[:, 1:2], bn_beta)
         for b in feature_blocks:
             rows = slice(b * P, (b + 1) * P)
             queues[b].dma_start(centres_sb[b][:], clusters2[rows, :])
@@ -83,14 +85,16 @@ def tile_modelnew_kernel(tc, base, x, clusters, clusters2, bn_gamma, bn_beta, of
                 nc.tensor.matmul(idle_ps[:], zeros[:], zeros[:], start=True, stop=True)
 
             z_ps = [front.tile([P, SAMPLE_TOKENS], F32, name=f"z_ps{i}") for i in samples]
-            stats = held.tile([P, SAMPLES, 6], F32, name="stats")
+            stats = held.tile([P, SAMPLES * 6 + 3], F32, name="stats")
+            nc.vector.memset(stats[:, SAMPLES * 6 : SAMPLES * 6 + 2], 0.0)
+            nc.vector.memset(stats[:, SAMPLES * 6 + 2 : SAMPLES * 6 + 3], BN_EPS * TOKENS)
             for i in samples:
                 for b in feature_blocks:
                     nc.tensor.matmul(
                         z_ps[i][:], clusters_sb[b][:], x_sb[b][:, i * SAMPLE_TOKENS : (i + 1) * SAMPLE_TOKENS],
                         start=(b == 0), stop=(b == FEATURE_BLOCKS - 1),
                     )
-                nc.vector.bn_stats(stats[:, i, :], z_ps[i][:])
+                nc.vector.bn_stats(stats[:, i * 6 : (i + 1) * 6], z_ps[i][:])
 
             xT_ps = front.tile([P, TOKEN_BLOCKS, FEATURES], BF16, name="xT_ps")
             for t in token_blocks:
@@ -101,24 +105,20 @@ def tile_modelnew_kernel(tc, base, x, clusters, clusters2, bn_gamma, bn_beta, of
             nc.scalar.copy(xT_sb[:], xT_ps[:])
 
             mean_var = held.tile([P, 2], F32, name="mean_var")
-            nc.vector.bn_aggr(mean_var[:], stats[:].rearrange("p i s -> p (i s)"))
-            mean, var = mean_var[:, 0:1], mean_var[:, 1:2]
-            var_eps = held.tile([P, 1], F32, name="var_eps")
+            nc.vector.bn_aggr(mean_var[:], stats[:])
+            mean, var_eps = mean_var[:, 0:1], mean_var[:, 1:2]
             rstd = held.tile([P, 1], F32, name="rstd")
-            neg_mean_gamma = held.tile([P, 1], F32, name="neg_mean_gamma")
-            scale = held.tile([P, 1], F32, name="scale")
-            shift = held.tile([P, 1], F32, name="shift")
-            nc.vector.tensor_scalar_add(var_eps[:], var, BN_EPS)
-            nc.gpsimd.tensor_tensor(rstd[:], var_eps[:], minus_half[:], ALU.pow)
-            nc.vector.tensor_scalar(neg_mean_gamma[:], mean, gamma[:], -1.0, op0=ALU.mult, op1=ALU.mult)
-            nc.vector.tensor_mul(scale[:], gamma[:], rstd[:])
-            nc.vector.tensor_scalar(shift[:], neg_mean_gamma[:], rstd[:], beta[:], op0=ALU.mult, op1=ALU.add)
+            scale_shift = held.tile([P, 2], F32, name="scale_shift")
+            scale, shift = scale_shift[:, 0:1], scale_shift[:, 1:2]
+            nc.gpsimd.tensor_tensor(rstd[:], var_eps, minus_half[:], ALU.pow)
+            nc.vector.tensor_scalar(neg_mean_gamma, mean, gamma, -1.0, op0=ALU.mult, op1=ALU.mult)
+            nc.vector.scalar_tensor_tensor(scale_shift[:], factors[:], rstd[:], addends[:], op0=ALU.mult, op1=ALU.add)
 
             for t in token_blocks:
                 sample, step = divmod(t, BLOCKS_PER_SAMPLE)
                 block = slice(t * P, (t + 1) * P)
                 nc.vector.tensor_scalar(
-                    y_sb[:, block], z_ps[sample][:, step * P : (step + 1) * P], scale[:], shift[:],
+                    y_sb[:, block], z_ps[sample][:, step * P : (step + 1) * P], scale, shift,
                     op0=ALU.mult, op1=ALU.add,
                 )
                 nc.tensor.transpose(yT_ps[t][:], y_sb[:, block], identity_f32[:])

@@ -68,8 +68,8 @@ def tile_modelnew_kernel(tc, base, x, clusters, clusters2, bn_gamma, bn_beta, of
         nc.gpsimd.memset(zeros[:], 0.0)
         nc.vector.memset(ones[:], 1.0)
         nc.vector.memset(minus_half[:], -0.5)
+        make_identity(nc, identity_bf16[:])
         make_identity(nc, identity_f32[:])
-        nc.vector.tensor_copy(identity_bf16[:], identity_f32[:])
 
         neg_centres = [held.tile([P, CLUSTERS], F32, name=f"neg_centres{b}") for b in feature_blocks]
         for b in feature_blocks:
@@ -104,6 +104,9 @@ def tile_modelnew_kernel(tc, base, x, clusters, clusters2, bn_gamma, bn_beta, of
                     )
             nc.scalar.copy(xT_sb[:], xT_ps[:])
 
+            for r in range(KEEP_WARM_MATMULS):
+                nc.tensor.matmul(idle_ps[:], zeros[:], x_sb[0][:, 0:P], start=True, stop=True)
+
             mean_var = held.tile([P, 2], F32, name="mean_var")
             nc.vector.bn_aggr(mean_var[:], stats[:])
             mean, var_eps = mean_var[:, 0:1], mean_var[:, 1:2]
@@ -124,7 +127,7 @@ def tile_modelnew_kernel(tc, base, x, clusters, clusters2, bn_gamma, bn_beta, of
                 nc.tensor.transpose(yT_ps[t][:], y_sb[:, block], identity_f32[:])
 
             for r in range(KEEP_WARM_MATMULS):
-                nc.tensor.matmul(idle_ps[:], zeros[:], xT_sb[:, 0, 0:P], start=True, stop=True)
+                nc.tensor.matmul(z_ps[1][:, 0:P], zeros[:], x_sb[0][:, 0:P], start=True, stop=True)
 
         with tc.psum_pool(name="back", bufs=1) as back:
             e_sb, e_sum, asgT = [], [], []

@@ -42,10 +42,8 @@ def tile_modelnew_kernel(tc, base, x, clusters, clusters2, bn_gamma, bn_beta, of
         clusters_sb = [held.tile([P, CLUSTERS], BF16, name=f"clusters_sb{b}") for b in feature_blocks]
         centres_sb = [held.tile([P, CLUSTERS], F32, name=f"centres_sb{b}") for b in feature_blocks]
         window = [held.tile([P, BANK], F32, name=f"window{b}") for b in feature_blocks]
-        factors = held.tile([P, 2], F32, name="factors")
-        addends = held.tile([P, 2], F32, name="addends")
-        gamma, neg_mean_gamma = factors[:, 0:1], factors[:, 1:2]
-        nc.vector.memset(addends[:], 0.0)
+        gamma = held.tile([P, 1], F32, name="gamma")
+        beta = held.tile([P, 1], F32, name="beta")
 
         queues = [nc.sync, nc.scalar]
         for b in feature_blocks:
@@ -53,8 +51,8 @@ def tile_modelnew_kernel(tc, base, x, clusters, clusters2, bn_gamma, bn_beta, of
             queues[b].dma_start(clusters_sb[b][:], clusters[rows, :])
             queues[b].dma_start(x_sb[b][:], x[rows, :])
         nc.sync.dma_start(offsets[:], offs)
-        nc.scalar.dma_start(gamma, bn_gamma)
-        nc.scalar.dma_start(addends[:, 1:2], bn_beta)
+        nc.scalar.dma_start(gamma[:], bn_gamma)
+        nc.scalar.dma_start(beta[:], bn_beta)
         for b in feature_blocks:
             rows = slice(b * P, (b + 1) * P)
             queues[b].dma_start(centres_sb[b][:], clusters2[rows, :])
@@ -111,23 +109,21 @@ def tile_modelnew_kernel(tc, base, x, clusters, clusters2, bn_gamma, bn_beta, of
             nc.vector.bn_aggr(mean_var[:], stats[:])
             mean, var_eps = mean_var[:, 0:1], mean_var[:, 1:2]
             rstd = held.tile([P, 1], F32, name="rstd")
-            scale_shift = held.tile([P, 2], F32, name="scale_shift")
-            scale, shift = scale_shift[:, 0:1], scale_shift[:, 1:2]
             nc.gpsimd.tensor_tensor(rstd[:], var_eps, minus_half[:], ALU.pow)
-            nc.vector.tensor_scalar(neg_mean_gamma, mean, gamma, -1.0, op0=ALU.mult, op1=ALU.mult)
-            nc.vector.scalar_tensor_tensor(scale_shift[:], factors[:], rstd[:], addends[:], op0=ALU.mult, op1=ALU.add)
+            centred = held.tile([P, TOKENS], F32, name="centred")
+            for i in samples:
+                nc.vector.tensor_scalar(
+                    centred[:, i * SAMPLE_TOKENS : (i + 1) * SAMPLE_TOKENS], z_ps[i][:], mean, gamma[:],
+                    op0=ALU.subtract, op1=ALU.mult,
+                )
 
             for t in token_blocks:
-                sample, step = divmod(t, BLOCKS_PER_SAMPLE)
                 block = slice(t * P, (t + 1) * P)
-                nc.vector.tensor_scalar(
-                    y_sb[:, block], z_ps[sample][:, step * P : (step + 1) * P], scale, shift,
-                    op0=ALU.mult, op1=ALU.add,
-                )
+                nc.vector.tensor_scalar(y_sb[:, block], centred[:, block], rstd[:], beta[:], op0=ALU.mult, op1=ALU.add)
                 nc.tensor.transpose(yT_ps[t][:], y_sb[:, block], identity_f32[:])
 
-            for r in range(KEEP_WARM_MATMULS):
-                nc.tensor.matmul(z_ps[1][:, 0:P], zeros[:], x_sb[0][:, 0:P], start=True, stop=True)
+            for r in range(KEEP_WARM_MATMULS // 4):
+                nc.tensor.matmul(idle_ps[:], identity_f32[:], y_sb[:, (TOKEN_BLOCKS - 1) * P :], start=True, stop=True)
 
         with tc.psum_pool(name="back", bufs=1) as back:
             e_sb, e_sum, asgT = [], [], []

@@ -20,7 +20,7 @@ TOKEN_BLOCKS = TOKENS // P
 BLOCKS_PER_SAMPLE = TOKEN_BLOCKS // SAMPLES
 SAMPLE_TOKENS = TOKENS // SAMPLES
 
-WARM_UP_MATMULS = 16
+WARM_UP_MATMULS = 12
 KEEP_WARM_MATMULS = 8
 
 FLOPS = 2 * 2 * FEATURES * CLUSTERS * TOKENS
@@ -49,7 +49,7 @@ def tile_modelnew_kernel(tc, base, x, clusters, clusters2, bn_gamma, bn_beta, of
         for b in feature_blocks:
             rows = slice(b * P, (b + 1) * P)
             queues[b].dma_start(clusters_sb[b][:], clusters[rows, :])
-            queues[b].dma_start(x_sb[b][:], x[rows, :])
+            queues[1 - b].dma_start(x_sb[b][:], x[rows, :])
         nc.sync.dma_start(offsets[:], offs)
         nc.scalar.dma_start(gamma[:], bn_gamma)
         nc.scalar.dma_start(beta[:], bn_beta)
@@ -62,8 +62,9 @@ def tile_modelnew_kernel(tc, base, x, clusters, clusters2, bn_gamma, bn_beta, of
         identity_bf16 = held.tile([P, P], BF16, name="identity_bf16")
         ones = held.tile([P, P], BF16, name="ones")
         minus_half = held.tile([P, 1], F32, name="minus_half")
-        zeros = held.tile([P, P], BF16, name="zeros")
-        nc.gpsimd.memset(zeros[:], 0.0)
+        zero_words = held.tile([P, P // 2], F32, name="zero_words")
+        nc.gpsimd.memset(zero_words[:], 0.0)
+        zeros = zero_words[:].bitcast(BF16)
         nc.vector.memset(ones[:], 1.0)
         nc.vector.memset(minus_half[:], -0.5)
         make_identity(nc, identity_bf16[:])
@@ -80,18 +81,19 @@ def tile_modelnew_kernel(tc, base, x, clusters, clusters2, bn_gamma, bn_beta, of
         with tc.psum_pool(name="front", bufs=1) as front:
             idle_ps = front.tile([P, P], F32, name="idle_ps")
             for r in range(WARM_UP_MATMULS):
-                nc.tensor.matmul(idle_ps[:], zeros[:], zeros[:], start=True, stop=True)
+                nc.tensor.matmul(idle_ps[:], zeros, zeros, start=True, stop=True)
 
             z_ps = [front.tile([P, SAMPLE_TOKENS], F32, name=f"z_ps{i}") for i in samples]
             stats = held.tile([P, SAMPLES * 6 + 3], F32, name="stats")
             nc.vector.memset(stats[:, SAMPLES * 6 : SAMPLES * 6 + 2], 0.0)
             nc.vector.memset(stats[:, SAMPLES * 6 + 2 : SAMPLES * 6 + 3], BN_EPS * TOKENS)
-            for i in samples:
-                for b in feature_blocks:
+            for b in feature_blocks:
+                for i in samples:
                     nc.tensor.matmul(
                         z_ps[i][:], clusters_sb[b][:], x_sb[b][:, i * SAMPLE_TOKENS : (i + 1) * SAMPLE_TOKENS],
                         start=(b == 0), stop=(b == FEATURE_BLOCKS - 1),
                     )
+            for i in samples:
                 nc.vector.bn_stats(stats[:, i * 6 : (i + 1) * 6], z_ps[i][:])
 
             xT_ps = front.tile([P, TOKEN_BLOCKS, FEATURES], BF16, name="xT_ps")
@@ -103,7 +105,7 @@ def tile_modelnew_kernel(tc, base, x, clusters, clusters2, bn_gamma, bn_beta, of
             nc.scalar.copy(xT_sb[:], xT_ps[:])
 
             for r in range(KEEP_WARM_MATMULS):
-                nc.tensor.matmul(idle_ps[:], zeros[:], x_sb[0][:, 0:P], start=True, stop=True)
+                nc.tensor.matmul(idle_ps[:], zeros, x_sb[1][:, 0:P], start=True, stop=True)
 
             mean_var = held.tile([P, 2], F32, name="mean_var")
             nc.vector.bn_aggr(mean_var[:], stats[:])
@@ -140,29 +142,27 @@ def tile_modelnew_kernel(tc, base, x, clusters, clusters2, bn_gamma, bn_beta, of
                 nc.vector.tensor_scalar_mul(asgT[t][:], e_sb[t][:], inv_sum[:])
 
             asum_ps = [back.tile([P, CLUSTERS], F32, name=f"asum_ps{i}") for i in samples]
-            agg_ps = [back.tile([P, LISTED], F32, name=f"agg_ps{b}") for b in feature_blocks]
+            agg_first_ps = [back.tile([P, CLUSTERS], F32, name=f"agg_first_ps{i}") for i in samples]
+            agg_second_ps = flipped.tile([P, LISTED], F32, name="agg_second_ps", tag="yT_ps")
+            agg_sb = [held.tile([P, LISTED], F32, name=f"agg_sb{b}") for b in feature_blocks]
             neg = [held.tile([P, LISTED], F32, name=f"neg{b}") for b in feature_blocks]
-            def agg_matmul(b, t):
-                sample, step = divmod(t, BLOCKS_PER_SAMPLE)
-                nc.tensor.matmul(
-                    agg_ps[b][:, sample * CLUSTERS : (sample + 1) * CLUSTERS], xT_sb[:, t, b * P : (b + 1) * P], asgT[t][:],
-                    start=(step == 0), stop=(step == BLOCKS_PER_SAMPLE - 1),
-                )
-
             for t in token_blocks:
                 sample, step = divmod(t, BLOCKS_PER_SAMPLE)
                 columns = slice(sample * CLUSTERS, (sample + 1) * CLUSTERS)
                 first, last = step == 0, step == BLOCKS_PER_SAMPLE - 1
                 nc.tensor.matmul(asum_ps[sample][:], ones[:], asgT[t][:], start=first, stop=last)
-                agg_matmul(0, t)
+                nc.tensor.matmul(agg_first_ps[sample][:], xT_sb[:, t, 0:P], asgT[t][:], start=first, stop=last)
                 if last:
+                    nc.scalar.copy(agg_sb[0][:, columns], agg_first_ps[sample][:])
                     for b in feature_blocks:
                         nc.vector.tensor_mul(neg[b][:, columns], asum_ps[sample][:], neg_centres[b][:])
             for t in token_blocks:
-                agg_matmul(1, t)
+                sample, step = divmod(t, BLOCKS_PER_SAMPLE)
+                columns = slice(sample * CLUSTERS, (sample + 1) * CLUSTERS)
+                first, last = step == 0, step == BLOCKS_PER_SAMPLE - 1
+                nc.tensor.matmul(agg_second_ps[:, columns], xT_sb[:, t, P:], asgT[t][:], start=first, stop=last)
+            nc.scalar.copy(agg_sb[1][:], agg_second_ps[:])
 
             for b in feature_blocks:
-                agg_sb = held.tile([P, LISTED], F32, name=f"agg_sb{b}")
-                nc.scalar.copy(agg_sb[:], agg_ps[b][:])
-                nc.vector.tensor_tensor(window[b][:].indirect(offsets[:]), agg_sb[:], neg[b][:], ALU.add)
+                nc.vector.tensor_tensor(window[b][:].indirect(offsets[:]), agg_sb[b][:], neg[b][:], ALU.add)
                 nc.sync.dma_start(out[b * P : (b + 1) * P, :], window[b][:])

@@ -46,10 +46,12 @@ def tile_modelnew_kernel(tc, base, x, clusters, clusters2, bn_gamma, bn_beta, of
         beta = held.tile([P, 1], F32, name="beta")
 
         queues = [nc.sync, nc.scalar]
+        x_pieces = [[slice(0, TOKENS)], [slice(0, SAMPLE_TOKENS), slice(SAMPLE_TOKENS, TOKENS)]]
         for b in feature_blocks:
             rows = slice(b * P, (b + 1) * P)
             queues[b].dma_start(clusters_sb[b][:], clusters[rows, :])
-            queues[1 - b].dma_start(x_sb[b][:], x[rows, :])
+            for tokens in x_pieces[b]:
+                queues[1 - b].dma_start(x_sb[b][:, tokens], x[rows, tokens])
         nc.sync.dma_start(offsets[:], offs)
         nc.scalar.dma_start(gamma[:], bn_gamma)
         nc.scalar.dma_start(beta[:], bn_beta)
@@ -105,7 +107,7 @@ def tile_modelnew_kernel(tc, base, x, clusters, clusters2, bn_gamma, bn_beta, of
             nc.scalar.copy(xT_sb[:], xT_ps[:])
 
             for r in range(KEEP_WARM_MATMULS):
-                nc.tensor.matmul(idle_ps[:], zeros, x_sb[1][:, 0:P], start=True, stop=True)
+                nc.tensor.matmul(idle_ps[:], zeros, x_sb[1][:, TOKENS - P :], start=True, stop=True)
 
             mean_var = held.tile([P, 2], F32, name="mean_var")
             nc.vector.bn_aggr(mean_var[:], stats[:])

@@ -46,11 +46,12 @@ def tile_modelnew_kernel(tc, base, x, clusters, clusters2, bn_gamma, bn_beta, of
         beta = held.tile([P, 1], F32, name="beta")
 
         queues = [nc.sync, nc.scalar]
-        x_pieces = [[slice(0, TOKENS)], [slice(0, SAMPLE_TOKENS), slice(SAMPLE_TOKENS, TOKENS)]]
-        for b in feature_blocks:
-            rows = slice(b * P, (b + 1) * P)
-            queues[b].dma_start(clusters_sb[b][:], clusters[rows, :])
-            for tokens in x_pieces[b]:
+        for i in samples:
+            tokens = slice(i * SAMPLE_TOKENS, (i + 1) * SAMPLE_TOKENS)
+            for b in feature_blocks:
+                rows = slice(b * P, (b + 1) * P)
+                if i == 0:
+                    queues[b].dma_start(clusters_sb[b][:], clusters[rows, :])
                 queues[1 - b].dma_start(x_sb[b][:, tokens], x[rows, tokens])
         nc.sync.dma_start(offsets[:], offs)
         nc.scalar.dma_start(gamma[:], bn_gamma)
@@ -89,13 +90,12 @@ def tile_modelnew_kernel(tc, base, x, clusters, clusters2, bn_gamma, bn_beta, of
             stats = held.tile([P, SAMPLES * 6 + 3], F32, name="stats")
             nc.vector.memset(stats[:, SAMPLES * 6 : SAMPLES * 6 + 2], 0.0)
             nc.vector.memset(stats[:, SAMPLES * 6 + 2 : SAMPLES * 6 + 3], BN_EPS * TOKENS)
-            for b in feature_blocks:
-                for i in samples:
+            for i in samples:
+                for b in feature_blocks:
                     nc.tensor.matmul(
                         z_ps[i][:], clusters_sb[b][:], x_sb[b][:, i * SAMPLE_TOKENS : (i + 1) * SAMPLE_TOKENS],
                         start=(b == 0), stop=(b == FEATURE_BLOCKS - 1),
                     )
-            for i in samples:
                 nc.vector.bn_stats(stats[:, i * 6 : (i + 1) * 6], z_ps[i][:])
 
             xT_ps = front.tile([P, TOKEN_BLOCKS, FEATURES], BF16, name="xT_ps")
@@ -106,8 +106,9 @@ def tile_modelnew_kernel(tc, base, x, clusters, clusters2, bn_gamma, bn_beta, of
                     )
             nc.scalar.copy(xT_sb[:], xT_ps[:])
 
+            last_piece = slice(TOKENS - P, TOKENS)
             for r in range(KEEP_WARM_MATMULS):
-                nc.tensor.matmul(idle_ps[:], zeros, x_sb[1][:, TOKENS - P :], start=True, stop=True)
+                nc.tensor.matmul(idle_ps[:], x_sb[0][:, last_piece], x_sb[1][:, last_piece], start=True, stop=True)
 
             mean_var = held.tile([P, 2], F32, name="mean_var")
             nc.vector.bn_aggr(mean_var[:], stats[:])

@@ -21,7 +21,8 @@ BLOCKS_PER_SAMPLE = TOKEN_BLOCKS // SAMPLES
 SAMPLE_TOKENS = TOKENS // SAMPLES
 
 WARM_UP_MATMULS = 12
-KEEP_WARM_MATMULS = 8
+KEEP_WARM_MATMULS = 12
+LATE_WARM_MATMULS = 2
 
 FLOPS = 2 * 2 * FEATURES * CLUSTERS * TOKENS
 
@@ -122,12 +123,14 @@ def tile_modelnew_kernel(tc, base, x, clusters, clusters2, bn_gamma, bn_beta, of
                     op0=ALU.subtract, op1=ALU.mult,
                 )
 
+            nc.tensor.matmul(idle_ps[:], identity_f32[:], centred[:, 0:P], start=True, stop=True)
+
             for t in token_blocks:
                 block = slice(t * P, (t + 1) * P)
                 nc.vector.tensor_scalar(y_sb[:, block], centred[:, block], rstd[:], beta[:], op0=ALU.mult, op1=ALU.add)
                 nc.tensor.transpose(yT_ps[t][:], y_sb[:, block], identity_f32[:])
 
-            for r in range(KEEP_WARM_MATMULS // 4):
+            for r in range(LATE_WARM_MATMULS):
                 nc.tensor.matmul(idle_ps[:], identity_f32[:], y_sb[:, (TOKEN_BLOCKS - 1) * P :], start=True, stop=True)
 
         with tc.psum_pool(name="back", bufs=1) as back:

@@ -83,19 +83,19 @@ def tile_modelnew_kernel(tc, base, x, clusters, clusters2, bn_gamma, bn_beta, of
         yT_ps = [flipped.tile([P, CLUSTERS], F32, name="yT_ps") for t in token_blocks]
 
         with tc.psum_pool(name="front", bufs=1) as front:
-            idle_ps = front.tile([P, P], F32, name="idle_ps")
             for r in range(WARM_UP_MATMULS):
-                nc.tensor.matmul(idle_ps[:], zeros, zeros, start=True, stop=True)
+                nc.tensor.matmul(yT_ps[-1][:], zeros, zeros, start=True, stop=True)
 
-            z_ps = [front.tile([P, SAMPLE_TOKENS], F32, name=f"z_ps{i}") for i in samples]
-            stats = held.tile([P, SAMPLES * 6 + 3], F32, name="stats")
-            nc.vector.memset(stats[:, SAMPLES * 6 : SAMPLES * 6 + 2], 0.0)
-            nc.vector.memset(stats[:, SAMPLES * 6 + 2 : SAMPLES * 6 + 3], BN_EPS * TOKENS)
-            for i in samples:
+            chunks = [slice(0, 2 * P), slice(2 * P, 3 * P), slice(3 * P, 4 * P)]
+            z_ps = [front.tile([P, c.stop - c.start], F32, name=f"z_ps{i}") for i, c in enumerate(chunks)]
+            filled = len(chunks) * 6
+            stats = held.tile([P, filled + 3], F32, name="stats")
+            nc.vector.memset(stats[:, filled : filled + 2], 0.0)
+            nc.vector.memset(stats[:, filled + 2 : filled + 3], BN_EPS * TOKENS)
+            for i, chunk in enumerate(chunks):
                 for b in feature_blocks:
                     nc.tensor.matmul(
-                        z_ps[i][:], clusters_sb[b][:], x_sb[b][:, i * SAMPLE_TOKENS : (i + 1) * SAMPLE_TOKENS],
-                        start=(b == 0), stop=(b == FEATURE_BLOCKS - 1),
+                        z_ps[i][:], clusters_sb[b][:], x_sb[b][:, chunk], start=(b == 0), stop=(b == FEATURE_BLOCKS - 1)
                     )
                 nc.vector.bn_stats(stats[:, i * 6 : (i + 1) * 6], z_ps[i][:])
 
@@ -109,7 +109,7 @@ def tile_modelnew_kernel(tc, base, x, clusters, clusters2, bn_gamma, bn_beta, of
 
             last_piece = slice(TOKENS - P, TOKENS)
             for r in range(KEEP_WARM_MATMULS):
-                nc.tensor.matmul(idle_ps[:], x_sb[0][:, last_piece], x_sb[1][:, last_piece], start=True, stop=True)
+                nc.tensor.matmul(yT_ps[-1][:], x_sb[0][:, last_piece], x_sb[1][:, last_piece], start=True, stop=True)
 
             mean_var = held.tile([P, 2], F32, name="mean_var")
             nc.vector.bn_aggr(mean_var[:], stats[:])
@@ -117,19 +117,19 @@ def tile_modelnew_kernel(tc, base, x, clusters, clusters2, bn_gamma, bn_beta, of
             rstd = held.tile([P, 1], F32, name="rstd")
             nc.gpsimd.tensor_tensor(rstd[:], var_eps, minus_half[:], ALU.pow)
             centred = held.tile([P, TOKENS], F32, name="centred")
-            for i in samples:
+            for i, chunk in enumerate(chunks):
                 nc.vector.tensor_scalar(
-                    centred[:, i * SAMPLE_TOKENS : (i + 1) * SAMPLE_TOKENS], z_ps[i][:], mean, gamma[:],
-                    op0=ALU.subtract, op1=ALU.mult,
+                    centred[:, chunk], z_ps[i][:], mean, gamma[:], op0=ALU.subtract, op1=ALU.mult
                 )
 
-            nc.tensor.matmul(idle_ps[:], identity_f32[:], centred[:, 0:P], start=True, stop=True)
+            nc.tensor.matmul(yT_ps[-1][:], identity_f32[:], centred[:, 0:P], start=True, stop=True)
 
             for t in token_blocks:
                 block = slice(t * P, (t + 1) * P)
                 nc.vector.tensor_scalar(y_sb[:, block], centred[:, block], rstd[:], beta[:], op0=ALU.mult, op1=ALU.add)
                 nc.tensor.transpose(yT_ps[t][:], y_sb[:, block], identity_f32[:])
 
+            idle_ps = front.tile([P, P], F32, name="idle_ps", tag="z_ps0")
             for r in range(LATE_WARM_MATMULS):
                 nc.tensor.matmul(idle_ps[:], identity_f32[:], y_sb[:, (TOKEN_BLOCKS - 1) * P :], start=True, stop=True)
 

import concourse.mybir as mybir
from concourse.masks import make_identity

F32, BF16, U16 = mybir.dt.float32, mybir.dt.bfloat16, mybir.dt.uint16
ALU = mybir.AluOpType
ACT = mybir.ActivationFunctionType
AXIS = mybir.AxisListType

P = 128
SAMPLES = 2
TOKENS = 512
FEATURES = 256
CLUSTERS = 128
BANK = 512
LISTED = 256
BN_EPS = 1e-5

FEATURE_BLOCKS = FEATURES // P
TOKEN_BLOCKS = TOKENS // P
BLOCKS_PER_SAMPLE = TOKEN_BLOCKS // SAMPLES
SAMPLE_TOKENS = TOKENS // SAMPLES

WARM_UP_MATMULS = 12
KEEP_WARM_MATMULS = 12
LATE_WARM_MATMULS = 2

FLOPS = 2 * 2 * FEATURES * CLUSTERS * TOKENS


def tile_modelnew_kernel(tc, base, x, clusters, clusters2, bn_gamma, bn_beta, offs, out):
    nc = tc.nc
    feature_blocks = range(FEATURE_BLOCKS)
    token_blocks = range(TOKEN_BLOCKS)
    samples = range(SAMPLES)

    with (
        tc.tile_pool(name="held", bufs=1) as held,
        tc.tile_pool(name="per_block", bufs=TOKEN_BLOCKS) as per_block,
        tc.psum_pool(name="flipped", bufs=TOKEN_BLOCKS) as flipped,
    ):
        offsets = held.tile([P, LISTED // 16], U16, name="offsets")
        x_sb = [held.tile([P, TOKENS], BF16, name=f"x_sb{b}") for b in feature_blocks]
        clusters_sb = [held.tile([P, CLUSTERS], BF16, name=f"clusters_sb{b}") for b in feature_blocks]
        centres_sb = [held.tile([P, CLUSTERS], F32, name=f"centres_sb{b}") for b in feature_blocks]
        window = [held.tile([P, BANK], F32, name=f"window{b}") for b in feature_blocks]
        gamma = held.tile([P, 1], F32, name="gamma")
        beta = held.tile([P, 1], F32, name="beta")

        queues = [nc.sync, nc.scalar]
        for i in samples:
            tokens = slice(i * SAMPLE_TOKENS, (i + 1) * SAMPLE_TOKENS)
            for b in feature_blocks:
                rows = slice(b * P, (b + 1) * P)
                if i == 0:
                    queues[b].dma_start(clusters_sb[b][:], clusters[rows, :])
                queues[1 - b].dma_start(x_sb[b][:, tokens], x[rows, tokens])
        nc.sync.dma_start(offsets[:], offs)
        nc.scalar.dma_start(gamma[:], bn_gamma)
        nc.scalar.dma_start(beta[:], bn_beta)
        for b in feature_blocks:
            rows = slice(b * P, (b + 1) * P)
            queues[b].dma_start(centres_sb[b][:], clusters2[rows, :])
            queues[b].dma_start(window[b][:], base[rows, :])

        identity_f32 = held.tile([P, P], F32, name="identity_f32")
        identity_bf16 = held.tile([P, P], BF16, name="identity_bf16")
        ones = held.tile([P, P], BF16, name="ones")
        minus_half = held.tile([P, 1], F32, name="minus_half")
        zero_words = held.tile([P, P // 2], F32, name="zero_words")
        nc.gpsimd.memset(zero_words[:], 0.0)
        zeros = zero_words[:].bitcast(BF16)
        nc.vector.memset(ones[:], 1.0)
        nc.vector.memset(minus_half[:], -0.5)
        make_identity(nc, identity_bf16[:])
        make_identity(nc, identity_f32[:])

        neg_centres = [held.tile([P, CLUSTERS], F32, name=f"neg_centres{b}") for b in feature_blocks]
        for b in feature_blocks:
            nc.scalar.mul(neg_centres[b][:], centres_sb[b][:], -1.0)

        y_sb = held.tile([P, TOKENS], F32, name="y_sb")
        xT_sb = held.tile([P, TOKEN_BLOCKS, FEATURES], BF16, name="xT_sb")
        yT_ps = [flipped.tile([P, CLUSTERS], F32, name="yT_ps") for t in token_blocks]

        with tc.psum_pool(name="front", bufs=1) as front:
            for r in range(WARM_UP_MATMULS):
                nc.tensor.matmul(yT_ps[-1][:], zeros, zeros, start=True, stop=True)

            chunks = [slice(0, 2 * P), slice(2 * P, 3 * P), slice(3 * P, 4 * P)]
            z_ps = [front.tile([P, c.stop - c.start], F32, name=f"z_ps{i}") for i, c in enumerate(chunks)]
            filled = len(chunks) * 6
            stats = held.tile([P, filled + 3], F32, name="stats")
            nc.vector.memset(stats[:, filled : filled + 2], 0.0)
            nc.vector.memset(stats[:, filled + 2 : filled + 3], BN_EPS * TOKENS)
            for i, chunk in enumerate(chunks):
                for b in feature_blocks:
                    nc.tensor.matmul(
                        z_ps[i][:], clusters_sb[b][:], x_sb[b][:, chunk], start=(b == 0), stop=(b == FEATURE_BLOCKS - 1)
                    )
                nc.vector.bn_stats(stats[:, i * 6 : (i + 1) * 6], z_ps[i][:])

            xT_ps = front.tile([P, TOKEN_BLOCKS, FEATURES], BF16, name="xT_ps")
            for t in token_blocks:
                for b in feature_blocks:
                    nc.tensor.transpose(
                        xT_ps[:, t, b * P : (b + 1) * P], x_sb[b][:, t * P : (t + 1) * P], identity_bf16[:]
                    )
            nc.scalar.copy(xT_sb[:], xT_ps[:])

            last_piece = slice(TOKENS - P, TOKENS)
            for r in range(KEEP_WARM_MATMULS):
                nc.tensor.matmul(yT_ps[-1][:], x_sb[0][:, last_piece], x_sb[1][:, last_piece], start=True, stop=True)

            mean_var = held.tile([P, 2], F32, name="mean_var")
            nc.vector.bn_aggr(mean_var[:], stats[:])
            mean, var_eps = mean_var[:, 0:1], mean_var[:, 1:2]
            rstd = held.tile([P, 1], F32, name="rstd")
            nc.gpsimd.tensor_tensor(rstd[:], var_eps, minus_half[:], ALU.pow)
            centred = held.tile([P, TOKENS], F32, name="centred")
            for i, chunk in enumerate(chunks):
                nc.vector.tensor_scalar(
                    centred[:, chunk], z_ps[i][:], mean, gamma[:], op0=ALU.subtract, op1=ALU.mult
                )

            nc.tensor.matmul(yT_ps[-1][:], identity_f32[:], centred[:, 0:P], start=True, stop=True)

            for t in token_blocks:
                block = slice(t * P, (t + 1) * P)
                nc.vector.tensor_scalar(y_sb[:, block], centred[:, block], rstd[:], beta[:], op0=ALU.mult, op1=ALU.add)
                nc.tensor.transpose(yT_ps[t][:], y_sb[:, block], identity_f32[:])

            idle_ps = front.tile([P, P], F32, name="idle_ps", tag="z_ps0")
            for r in range(LATE_WARM_MATMULS):
                nc.tensor.matmul(idle_ps[:], identity_f32[:], y_sb[:, (TOKEN_BLOCKS - 1) * P :], start=True, stop=True)

        with tc.psum_pool(name="back", bufs=1) as back:
            e_sb, e_sum, asgT = [], [], []
            for t in token_blocks:
                neg_max = per_block.tile([P, 1], F32, name="neg_max")
                e_sb.append(per_block.tile([P, CLUSTERS], F32, name="e_sb"))
                e_sum.append(per_block.tile([P, 1], F32, name="e_sum"))
                nc.vector.tensor_reduce(neg_max[:], yT_ps[t][:], axis=AXIS.X, op=ALU.max, negate=True)
                nc.scalar.activation(e_sb[t][:], yT_ps[t][:], ACT.Exp, bias=neg_max[:], accum_out=e_sum[t][:])
            for t in token_blocks:
                inv_sum = per_block.tile([P, 1], F32, name="inv_sum")
                asgT.append(per_block.tile([P, CLUSTERS], BF16, name="asgT"))
                nc.vector.reciprocal(inv_sum[:], e_sum[t][:])
                nc.vector.tensor_scalar_mul(asgT[t][:], e_sb[t][:], inv_sum[:])

            asum_ps = [back.tile([P, CLUSTERS], F32, name=f"asum_ps{i}") for i in samples]
            agg_first_ps = [back.tile([P, CLUSTERS], F32, name=f"agg_first_ps{i}") for i in samples]
            agg_second_ps = flipped.tile([P, LISTED], F32, name="agg_second_ps", tag="yT_ps")
            agg_sb = [held.tile([P, LISTED], F32, name=f"agg_sb{b}") for b in feature_blocks]
            neg = [held.tile([P, LISTED], F32, name=f"neg{b}") for b in feature_blocks]
            for t in token_blocks:
                sample, step = divmod(t, BLOCKS_PER_SAMPLE)
                columns = slice(sample * CLUSTERS, (sample + 1) * CLUSTERS)
                first, last = step == 0, step == BLOCKS_PER_SAMPLE - 1
                nc.tensor.matmul(asum_ps[sample][:], ones[:], asgT[t][:], start=first, stop=last)
                nc.tensor.matmul(agg_first_ps[sample][:], xT_sb[:, t, 0:P], asgT[t][:], start=first, stop=last)
                if last:
                    nc.scalar.copy(agg_sb[0][:, columns], agg_first_ps[sample][:])
                    for b in feature_blocks:
                        nc.vector.tensor_mul(neg[b][:, columns], asum_ps[sample][:], neg_centres[b][:])
            for t in token_blocks:
                sample, step = divmod(t, BLOCKS_PER_SAMPLE)
                columns = slice(sample * CLUSTERS, (sample + 1) * CLUSTERS)
                first, last = step == 0, step == BLOCKS_PER_SAMPLE - 1
                nc.tensor.matmul(agg_second_ps[:, columns], xT_sb[:, t, P:], asgT[t][:], start=first, stop=last)
            nc.scalar.copy(agg_sb[1][:], agg_second_ps[:])

            for b in feature_blocks:
                nc.vector.tensor_tensor(window[b][:].indirect(offsets[:]), agg_sb[b][:], neg[b][:], ALU.add)
                nc.sync.dma_start(out[b * P : (b + 1) * P, :], window[b][:])
